import numpy as np
import ml_dtypes


def mxq(x, axis, fmt="e4m3"):
    dtype, down = {"e4m3": (ml_dtypes.float8_e4m3fn, 7), "e5m2": (ml_dtypes.float8_e5m2, 14)}[fmt]
    v = np.moveaxis(np.asarray(x, np.float32).astype(ml_dtypes.bfloat16).astype(np.float64), axis, -1)
    blocks = v.reshape(v.shape[:-1] + (-1, 32))
    amax = np.abs(blocks).max(-1, keepdims=True)
    byte = np.maximum(np.where(amax > 0, np.frexp(amax)[1] - 1 + 127, 0) - down, 1)
    scale = np.exp2(byte - 127.0)
    codes = (blocks / scale).astype(np.float32).astype(dtype).astype(np.float64)
    return np.moveaxis((codes * scale).reshape(v.shape), -1, axis)


WIDE = False


def mx_kscale(k):
    if not WIDE:
        return np.ones(k)
    levels = np.array([20, -20, 10, -10, 0])
    a = np.random.permutation(np.resize(levels, k // 512 * 4)).reshape(k // 512, 4)
    idx = np.arange(k)
    return np.exp2(a[idx // 512, idx % 128 // 32])


BF16 = ml_dtypes.bfloat16


def bf(x):
    return np.asarray(x, np.float32).astype(BF16)


def f64(x):
    return np.asarray(x).astype(np.float64)


B, I, O, G = 2048, 512, 512, 8
K = I * G


def bspline_basis(d):
    inner = 1.0 - 6.0 * d * d + 6.0 * d * d * d
    outer = 2.0 * (1.0 - d) ** 3
    return np.where(d < 0.5, inner, np.where(d < 1.0, outer, np.zeros_like(d)))


def bspline_slope(d):
    inner = -12.0 * d + 18.0 * d * d
    outer = -6.0 * (1.0 - d) ** 2
    return np.where(d < 0.5, inner, np.where(d < 1.0, outer, np.zeros_like(d)))


def setup_inputs():
    g = np.linspace(-1.0, 1.0, G)
    s = mx_kscale(O)
    x_norm = np.tanh(np.random.standard_normal((B, I)))
    spline_weight = np.random.standard_normal((O, I, G)) / np.sqrt(I) / s[:, None, None]
    base_activation = np.random.standard_normal((O, I)) * 4.0 / np.sqrt(I) / s[:, None]
    grid_points = g + 0.1 * (g[1] - g[0]) * np.random.standard_normal(G)
    grad_out = np.random.standard_normal((B, O)) * np.exp2(np.random.randint(-12, 1, (B, 1))) * 4.0 * s
    return {"x_norm": bf(x_norm),
            "spline_weight": bf(spline_weight),
            "base_activation": bf(base_activation),
            "grid_points": bf(grid_points),
            "grad_out": bf(grad_out)}


def reference(x_norm, spline_weight, base_activation, grid_points, grad_out):
    t = f64(x_norm)
    diff = t[:, :, None] - f64(grid_points)
    slope = bspline_slope(np.abs(diff)) * np.sign(diff)
    gq = mxq(f64(grad_out), 1, "e5m2")
    h = gq @ mxq(f64(spline_weight).reshape(O, K), 0, "e4m3")
    base = gq @ mxq(f64(base_activation), 0, "e4m3")
    return (h.reshape(B, I, G) * slope).sum(axis=2) + 0.1 * base

@@ -1,0 +1,241 @@
+from contextlib import ExitStack
+
+import concourse.mybir as mybir
+from concourse.masks import make_identity
+
+F32 = mybir.dt.float32
+BF16 = mybir.dt.bfloat16
+U32 = mybir.dt.uint32
+U8 = mybir.dt.uint8
+E4M3_X4 = mybir.dt.float8_e4m3fn_x4
+E5M2_X4 = mybir.dt.float8_e5m2_x4
+ALU = mybir.AluOpType
+ACT = mybir.ActivationFunctionType
+
+B, I, O, G = 2048, 512, 512, 8
+P = 128
+PACK = 4
+N_COLS = 512
+I_BLOCKS = I // P
+B_BLOCKS = B // N_COLS
+SUB = N_COLS // P
+TERMS = G + 1
+
+FLOPS = 2 * B * O * (I * G + I)
+
+
+def tile_advancedkanlayer_pa_kernel(
+    tc, x_norm, spline_weight, base_activation, grid_points, grad_out, out
+):
+    nc = tc.nc
+    with ExitStack() as ctx:
+        keep = ctx.enter_context(tc.tile_pool(name="keep", bufs=1))
+        stage = ctx.enter_context(tc.tile_pool(name="stage", bufs=1))
+        curves = ctx.enter_context(tc.tile_pool(name="curves", bufs=2))
+        single = ctx.enter_context(tc.tile_pool(name="single", bufs=1))
+        banks = ctx.enter_context(tc.psum_pool(name="banks", bufs=6))
+        sums = ctx.enter_context(tc.psum_pool(name="sums", bufs=2))
+
+        ident_bf16 = keep.tile([P, P], BF16)
+        make_identity(nc, ident_bf16[:])
+        ident_f32 = keep.tile([P, P], F32)
+        make_identity(nc, ident_f32[:])
+
+        knots_bf16 = keep.tile([P, G], BF16)
+        nc.sync.dma_start(out=knots_bf16[:], in_=grid_points.partition_broadcast(P))
+        knots = keep.tile([P, G], F32)
+        nc.vector.tensor_copy(out=knots[:], in_=knots_bf16[:])
+        neg_knots = keep.tile([P, G], F32)
+        nc.vector.tensor_scalar_mul(out=neg_knots[:], in0=knots_bf16[:], scalar1=-1.0)
+
+        g_codes = keep.tile([P, B], U32, align_bytes=64)
+        g_scales = keep.tile([P, B], U8, align_bytes=64)
+        w_codes = keep.tile([P, I_BLOCKS, TERMS, P], U32, align_bytes=64)
+        w_scales = keep.tile([P, I_BLOCKS, TERMS, P], U8, align_bytes=64)
+
+        x_rows = keep.tile([P, B // P, I], BF16)
+
+        def load_x(bq):
+            rows = slice(bq * N_COLS, (bq + 1) * N_COLS)
+            nc.sync.dma_start(
+                out=x_rows[:, bq * SUB : (bq + 1) * SUB, :],
+                in_=x_norm[rows, :].rearrange("(n p) i -> p n i", p=P),
+            )
+
+        def load_grad(bq):
+            rows = slice(bq * N_COLS, (bq + 1) * N_COLS)
+            g_rows = stage.tile([P, SUB, O], BF16, bufs=2)
+            nc.sync.dma_start(
+                out=g_rows[:], in_=grad_out[rows, :].rearrange("(n p) o -> p n o", p=P)
+            )
+            return g_rows
+
+        def quantise_grad(bq, g_rows):
+            g_grouped = stage.tile([P, N_COLS * PACK], BF16, align_bytes=64)
+            g_pairs = g_grouped[:].bitcast(F32).rearrange("p (n b u) -> p n b u", n=SUB, u=2)
+            for half in range(SUB // 2):
+                turned = banks.tile([P, 2, 2, P], F32, tag="bank")
+                for m in range(2):
+                    words = g_rows[:, 2 * half + m, :].bitcast(F32)
+                    words = words.rearrange("b (p u) -> b u p", u=2)
+                    for u in range(2):
+                        nc.tensor.transpose(turned[:, m, u, :], words[:, u, :], ident_f32[:])
+                nc.vector.tensor_copy(
+                    out=g_pairs[:, 2 * half : 2 * half + 2, :, :],
+                    in_=turned[:].rearrange("p m u b -> p m b u"),
+                )
+            cols = slice(bq * N_COLS, (bq + 1) * N_COLS)
+            nc.vector.quantize_mx(
+                out=g_codes[:, cols].bitcast(E5M2_X4), scales=g_scales[:, cols], in_=g_grouped[:]
+            )
+
+        def load_weights(k):
+            w_rows = stage.tile([P, PACK, TERMS * P], BF16, bufs=2)
+            nc.sync.dma_start(
+                out=w_rows[:, :, 0 : G * P],
+                in_=spline_weight.rearrange("(p j) i g -> p j (i g)", j=PACK)[
+                    :, :, k * G * P : (k + 1) * G * P
+                ],
+            )
+            nc.sync.dma_start(
+                out=w_rows[:, :, G * P : TERMS * P],
+                in_=base_activation.rearrange("(p j) i -> p j i", j=PACK)[
+                    :, :, k * P : (k + 1) * P
+                ],
+            )
+            return w_rows
+
+        def quantise_weights(k, w_rows):
+            w_grouped = stage.tile([P, TERMS, P, PACK], BF16, align_bytes=64)
+            nc.vector.tensor_copy(
+                out=w_grouped[:, 0:G, :, :],
+                in_=w_rows[:, :, 0 : G * P].rearrange("p j (i g) -> p g i j", g=G),
+            )
+            nc.vector.tensor_copy(
+                out=w_grouped[:, G, :, :],
+                in_=w_rows[:, :, G * P : TERMS * P].rearrange("p j i -> p i j"),
+            )
+            nc.vector.quantize_mx(
+                out=w_codes[:, k, 0:G, :].rearrange("p g i -> p (g i)").bitcast(E4M3_X4),
+                scales=w_scales[:, k, 0:G, :].rearrange("p g i -> p (g i)"),
+                in_=w_grouped[:, 0:G, :, :].rearrange("p g i j -> p (g i j)"),
+            )
+            nc.vector.quantize_mx(
+                out=w_codes[:, k, G, :].bitcast(E4M3_X4),
+                scales=w_scales[:, k, G, :],
+                in_=w_grouped[:, G, :, :].rearrange("p i j -> p (i j)"),
+            )
+
+        def curve_parts(k, bq):
+            x_turned = banks.tile([P, N_COLS], BF16, tag="bank")
+            for n in range(SUB):
+                nc.tensor.transpose(
+                    x_turned[:, n * P : (n + 1) * P],
+                    x_rows[:, bq * SUB + n, k * P : (k + 1) * P],
+                    ident_bf16[:],
+                )
+            x_cols = curves.tile([P, N_COLS], BF16)
+            nc.scalar.copy(out=x_cols[:], in_=x_turned[:])
+
+            dist = curves.tile([P, G, N_COLS], F32)
+            half_sign = curves.tile([P, G, N_COLS], BF16)
+            for g in range(G):
+                nc.scalar.activation(
+                    out=dist[:, g, :], in_=x_cols[:], func=ACT.Abs,
+                    bias=neg_knots[:, g : g + 1], scale=1.0,
+                )
+                nc.vector.tensor_scalar(
+                    out=half_sign[:, g, :], in0=x_cols[:],
+                    scalar1=knots[:, g : g + 1], scalar2=0.5,
+                    op0=ALU.is_gt, op1=ALU.subtract,
+                )
+            outer_sq = curves.tile([P, G, N_COLS], F32)
+            nc.vector.tensor_scalar(
+                out=outer_sq[:], in0=dist[:], scalar1=1.0, scalar2=1.0,
+                op0=ALU.min, op1=ALU.subtract,
+            )
+            inner_sq = curves.tile([P, G, N_COLS], F32)
+            nc.scalar.activation(
+                out=inner_sq[:], in_=dist[:], func=ACT.Relu, bias=1.0, scale=-2.0
+            )
+            nc.scalar.activation(out=inner_sq[:], in_=inner_sq[:], func=ACT.Square)
+            nc.scalar.activation(out=outer_sq[:], in_=outer_sq[:], func=ACT.Square)
+            return half_sign, inner_sq, outer_sq
+
+        def finish(k, bq, half_sign, inner_sq, outer_sq):
+            cols = slice(bq * N_COLS, (bq + 1) * N_COLS)
+            terms = single.tile([P, TERMS, N_COLS], F32)
+            nc.vector.tensor_tensor(
+                out=inner_sq[:], in0=inner_sq[:], in1=outer_sq[:], op=ALU.subtract
+            )
+            nc.vector.scalar_tensor_tensor(
+                out=terms[:, 0:G, :], in0=inner_sq[:], scalar=12.0, in1=half_sign[:],
+                op0=ALU.mult, op1=ALU.mult,
+            )
+            for t in range(TERMS):
+                h = banks.tile([P, N_COLS], F32, tag="bank")
+                nc.tensor.matmul_mx(
+                    out=h[:],
+                    lhsT=w_codes[:, k, t, :].bitcast(E4M3_X4),
+                    lhsT_scale=w_scales[:, k, t, :],
+                    rhs=g_codes[:, cols].bitcast(E5M2_X4),
+                    rhs_scale=g_scales[:, cols],
+                    start=True,
+                    stop=True,
+                )
+                if t < G:
+                    nc.vector.tensor_tensor(
+                        out=terms[:, t, :], in0=terms[:, t, :], in1=h[:], op=ALU.mult
+                    )
+                else:
+                    nc.scalar.mul(out=terms[:, t, :], in_=h[:], mul=0.1)
+            total = sums.tile([P, SUB, P], F32)
+            for s in range(SUB):
+                for t in range(TERMS):
+                    nc.tensor.matmul(
+                        out=total[:, s, :],
+                        lhsT=terms[:, t, s * P : (s + 1) * P],
+                        rhs=ident_f32[:],
+                        is_transpose=True,
+                        start=(t == 0),
+                        stop=(t == TERMS - 1),
+                    )
+            result = curves.tile([P, SUB, P], F32)
+            nc.scalar.copy(out=result[:], in_=total[:])
+            nc.sync.dma_start(
+                out=out[cols, k * P : (k + 1) * P].rearrange("(s p) i -> p s i", p=P),
+                in_=result[:],
+            )
+
+        units = [(k, bq) for k in range(I_BLOCKS) for bq in range(B_BLOCKS)]
+
+        g_loaded = {}
+        w_loaded = {}
+
+        def prepare(k, bq):
+            if k == 0:
+                quantise_grad(bq, g_loaded[bq])
+                if bq + 2 < B_BLOCKS:
+                    g_loaded[bq + 2] = load_grad(bq + 2)
+            if bq == 0:
+                quantise_weights(k, w_loaded[k])
+                if k + 2 < I_BLOCKS:
+                    w_loaded[k + 2] = load_weights(k + 2)
+
+        g_loaded[0] = load_grad(0)
+        load_x(0)
+        w_loaded[0] = load_weights(0)
+        g_loaded[1] = load_grad(1)
+        for bq in range(1, B_BLOCKS):
+            load_x(bq)
+        w_loaded[1] = load_weights(1)
+
+        prepare(*units[0])
+        parts = curve_parts(*units[0])
+        for u, unit in enumerate(units):
+            following = None
+            if u + 1 < len(units):
+                prepare(*units[u + 1])
+                following = curve_parts(*units[u + 1])
+            finish(*unit, *parts)
+            parts = following

@@ -32,7 +32,6 @@ def tile_advancedkanlayer_pa_kernel(
         keep = ctx.enter_context(tc.tile_pool(name="keep", bufs=1))
         stage = ctx.enter_context(tc.tile_pool(name="stage", bufs=1))
         curves = ctx.enter_context(tc.tile_pool(name="curves", bufs=2))
-        single = ctx.enter_context(tc.tile_pool(name="single", bufs=1))
         banks = ctx.enter_context(tc.psum_pool(name="banks", bufs=6))
         sums = ctx.enter_context(tc.psum_pool(name="sums", bufs=2))
 
@@ -45,8 +44,20 @@ def tile_advancedkanlayer_pa_kernel(
         nc.sync.dma_start(out=knots_bf16[:], in_=grid_points.partition_broadcast(P))
         knots = keep.tile([P, G], F32)
         nc.vector.tensor_copy(out=knots[:], in_=knots_bf16[:])
-        neg_knots = keep.tile([P, G], F32)
-        nc.vector.tensor_scalar_mul(out=neg_knots[:], in0=knots_bf16[:], scalar1=-1.0)
+        knots_less_1 = keep.tile([P, G], F32)
+        nc.vector.tensor_scalar_add(out=knots_less_1[:], in0=knots[:], scalar1=-1.0)
+        knots_plus_1 = keep.tile([P, G], F32)
+        nc.vector.tensor_scalar_add(out=knots_plus_1[:], in0=knots[:], scalar1=1.0)
+        half_less_knots = keep.tile([P, G], F32)
+        nc.vector.tensor_scalar(
+            out=half_less_knots[:], in0=knots[:], scalar1=-1.0, scalar2=0.5,
+            op0=ALU.mult, op1=ALU.add,
+        )
+        half_less_2_knots = keep.tile([P, G], F32)
+        nc.vector.tensor_scalar(
+            out=half_less_2_knots[:], in0=knots[:], scalar1=-2.0, scalar2=0.5,
+            op0=ALU.mult, op1=ALU.add,
+        )
 
         g_codes = keep.tile([P, B], U32, align_bytes=64)
         g_scales = keep.tile([P, B], U8, align_bytes=64)
@@ -126,7 +137,7 @@ def tile_advancedkanlayer_pa_kernel(
                 in_=w_grouped[:, G, :, :].rearrange("p i j -> p (i j)"),
             )
 
-        def curve_parts(k, bq):
+        def fold(k, bq):
             x_turned = banks.tile([P, N_COLS], BF16, tag="bank")
             for n in range(SUB):
                 nc.tensor.transpose(
@@ -136,42 +147,30 @@ def tile_advancedkanlayer_pa_kernel(
                 )
             x_cols = curves.tile([P, N_COLS], BF16)
             nc.scalar.copy(out=x_cols[:], in_=x_turned[:])
-
-            dist = curves.tile([P, G, N_COLS], F32)
-            half_sign = curves.tile([P, G, N_COLS], BF16)
+            clamped = curves.tile([P, G, N_COLS], F32)
+            folded = curves.tile([P, G, N_COLS], F32)
+            for g in range(G):
+                nc.vector.tensor_scalar(
+                    out=clamped[:, g, :], in0=x_cols[:],
+                    scalar1=knots_less_1[:, g : g + 1], scalar2=knots_plus_1[:, g : g + 1],
+                    op0=ALU.max, op1=ALU.min,
+                )
             for g in range(G):
                 nc.scalar.activation(
-                    out=dist[:, g, :], in_=x_cols[:], func=ACT.Abs,
-                    bias=neg_knots[:, g : g + 1], scale=1.0,
+                    out=folded[:, g, :], in_=clamped[:, g, :], func=ACT.Abs,
+                    bias=half_less_knots[:, g : g + 1], scale=1.0,
                 )
-                nc.vector.tensor_scalar(
-                    out=half_sign[:, g, :], in0=x_cols[:],
-                    scalar1=knots[:, g : g + 1], scalar2=0.5,
-                    op0=ALU.is_gt, op1=ALU.subtract,
-                )
-            outer_sq = curves.tile([P, G, N_COLS], F32)
-            nc.vector.tensor_scalar(
-                out=outer_sq[:], in0=dist[:], scalar1=1.0, scalar2=1.0,
-                op0=ALU.min, op1=ALU.subtract,
-            )
-            inner_sq = curves.tile([P, G, N_COLS], F32)
-            nc.scalar.activation(
-                out=inner_sq[:], in_=dist[:], func=ACT.Relu, bias=1.0, scale=-2.0
-            )
-            nc.scalar.activation(out=inner_sq[:], in_=inner_sq[:], func=ACT.Square)
-            nc.scalar.activation(out=outer_sq[:], in_=outer_sq[:], func=ACT.Square)
-            return half_sign, inner_sq, outer_sq
+            nc.scalar.activation(out=folded[:], in_=folded[:], func=ACT.Abs, bias=-1.0, scale=1.0)
+            return clamped, folded
 
-        def finish(k, bq, half_sign, inner_sq, outer_sq):
+        def products(k, bq, clamped, folded):
             cols = slice(bq * N_COLS, (bq + 1) * N_COLS)
-            terms = single.tile([P, TERMS, N_COLS], F32)
-            nc.vector.tensor_tensor(
-                out=inner_sq[:], in0=inner_sq[:], in1=outer_sq[:], op=ALU.subtract
-            )
+            both = curves.tile([P, G, N_COLS], F32)
             nc.vector.scalar_tensor_tensor(
-                out=terms[:, 0:G, :], in0=inner_sq[:], scalar=12.0, in1=half_sign[:],
-                op0=ALU.mult, op1=ALU.mult,
+                out=both[:], in0=clamped[:], scalar=2.0, in1=folded[:],
+                op0=ALU.mult, op1=ALU.subtract,
             )
+            terms = curves.tile([P, TERMS, N_COLS], F32)
             for t in range(TERMS):
                 h = banks.tile([P, N_COLS], F32, tag="bank")
                 nc.tensor.matmul_mx(
@@ -184,11 +183,25 @@ def tile_advancedkanlayer_pa_kernel(
                     stop=True,
                 )
                 if t < G:
-                    nc.vector.tensor_tensor(
-                        out=terms[:, t, :], in0=terms[:, t, :], in1=h[:], op=ALU.mult
+                    nc.vector.scalar_tensor_tensor(
+                        out=terms[:, t, :], in0=folded[:, t, :], scalar=0.5, in1=h[:],
+                        op0=ALU.subtract, op1=ALU.mult,
                     )
                 else:
-                    nc.scalar.mul(out=terms[:, t, :], in_=h[:], mul=0.1)
+                    nc.scalar.mul(out=terms[:, t, :], in_=h[:], mul=-0.1 / 6.0)
+            for g in range(G):
+                nc.scalar.activation(
+                    out=both[:, g, :], in_=both[:, g, :], func=ACT.Abs,
+                    bias=half_less_2_knots[:, g : g + 1], scale=1.0,
+                )
+            return both, terms
+
+        def finish(k, bq, both, terms):
+            cols = slice(bq * N_COLS, (bq + 1) * N_COLS)
+            nc.vector.scalar_tensor_tensor(
+                out=terms[:, 0:G, :], in0=both[:], scalar=2.0, in1=terms[:, 0:G, :],
+                op0=ALU.subtract, op1=ALU.mult,
+            )
             total = sums.tile([P, SUB, P], F32)
             for s in range(SUB):
                 for t in range(TERMS):
@@ -201,7 +214,7 @@ def tile_advancedkanlayer_pa_kernel(
                         stop=(t == TERMS - 1),
                     )
             result = curves.tile([P, SUB, P], F32)
-            nc.scalar.copy(out=result[:], in_=total[:])
+            nc.scalar.mul(out=result[:], in_=total[:], mul=-6.0)
             nc.sync.dma_start(
                 out=out[cols, k * P : (k + 1) * P].rearrange("(s p) i -> p s i", p=P),
                 in_=result[:],
@@ -230,12 +243,14 @@ def tile_advancedkanlayer_pa_kernel(
             load_x(bq)
         w_loaded[1] = load_weights(1)
 
-        prepare(*units[0])
-        parts = curve_parts(*units[0])
-        for u, unit in enumerate(units):
-            following = None
-            if u + 1 < len(units):
-                prepare(*units[u + 1])
-                following = curve_parts(*units[u + 1])
-            finish(*unit, *parts)
-            parts = following
+        n_units = len(units)
+        stage_a = {}
+        stage_b = {}
+        for step in range(n_units + 2):
+            if step < n_units:
+                prepare(*units[step])
+                stage_a[step] = fold(*units[step])
+            if 0 <= step - 1 < n_units:
+                stage_b[step - 1] = products(*units[step - 1], *stage_a[step - 1])
+            if 0 <= step - 2:
+                finish(*units[step - 2], *stage_b[step - 2])

@@ -33,7 +33,7 @@ def tile_advancedkanlayer_pa_kernel(
         stage = ctx.enter_context(tc.tile_pool(name="stage", bufs=1))
         curves = ctx.enter_context(tc.tile_pool(name="curves", bufs=2))
         banks = ctx.enter_context(tc.psum_pool(name="banks", bufs=6))
-        sums = ctx.enter_context(tc.psum_pool(name="sums", bufs=2))
+        sums = ctx.enter_context(tc.psum_pool(name="sums", bufs=1))
 
         ident_bf16 = keep.tile([P, P], BF16)
         make_identity(nc, ident_bf16[:])
@@ -44,10 +44,6 @@ def tile_advancedkanlayer_pa_kernel(
         nc.sync.dma_start(out=knots_bf16[:], in_=grid_points.partition_broadcast(P))
         knots = keep.tile([P, G], F32)
         nc.vector.tensor_copy(out=knots[:], in_=knots_bf16[:])
-        knots_less_1 = keep.tile([P, G], F32)
-        nc.vector.tensor_scalar_add(out=knots_less_1[:], in0=knots[:], scalar1=-1.0)
-        knots_plus_1 = keep.tile([P, G], F32)
-        nc.vector.tensor_scalar_add(out=knots_plus_1[:], in0=knots[:], scalar1=1.0)
         half_less_knots = keep.tile([P, G], F32)
         nc.vector.tensor_scalar(
             out=half_less_knots[:], in0=knots[:], scalar1=-1.0, scalar2=0.5,
@@ -147,30 +143,23 @@ def tile_advancedkanlayer_pa_kernel(
                 )
             x_cols = curves.tile([P, N_COLS], BF16)
             nc.scalar.copy(out=x_cols[:], in_=x_turned[:])
-            clamped = curves.tile([P, G, N_COLS], F32)
             folded = curves.tile([P, G, N_COLS], F32)
             for g in range(G):
-                nc.vector.tensor_scalar(
-                    out=clamped[:, g, :], in0=x_cols[:],
-                    scalar1=knots_less_1[:, g : g + 1], scalar2=knots_plus_1[:, g : g + 1],
-                    op0=ALU.max, op1=ALU.min,
-                )
-            for g in range(G):
                 nc.scalar.activation(
-                    out=folded[:, g, :], in_=clamped[:, g, :], func=ACT.Abs,
+                    out=folded[:, g, :], in_=x_cols[:], func=ACT.Abs,
                     bias=half_less_knots[:, g : g + 1], scale=1.0,
                 )
             nc.scalar.activation(out=folded[:], in_=folded[:], func=ACT.Abs, bias=-1.0, scale=1.0)
-            return clamped, folded
+            return x_cols, folded
 
-        def products(k, bq, clamped, folded):
+        def products(k, bq, x_cols, folded):
             cols = slice(bq * N_COLS, (bq + 1) * N_COLS)
-            both = curves.tile([P, G, N_COLS], F32)
+            reach = curves.tile([P, G, N_COLS], F32)
             nc.vector.scalar_tensor_tensor(
-                out=both[:], in0=clamped[:], scalar=2.0, in1=folded[:],
-                op0=ALU.mult, op1=ALU.subtract,
+                out=reach[:], in0=x_cols[:].unsqueeze(1).to_broadcast([P, G, N_COLS]),
+                scalar=2.0, in1=folded[:], op0=ALU.mult, op1=ALU.subtract,
             )
-            terms = curves.tile([P, TERMS, N_COLS], F32)
+            plain = curves.tile([P, TERMS, N_COLS], F32)
             for t in range(TERMS):
                 h = banks.tile([P, N_COLS], F32, tag="bank")
                 nc.tensor.matmul_mx(
@@ -184,37 +173,53 @@ def tile_advancedkanlayer_pa_kernel(
                 )
                 if t < G:
                     nc.vector.scalar_tensor_tensor(
-                        out=terms[:, t, :], in0=folded[:, t, :], scalar=0.5, in1=h[:],
+                        out=plain[:, t, :], in0=folded[:, t, :], scalar=0.5, in1=h[:],
                         op0=ALU.subtract, op1=ALU.mult,
                     )
                 else:
-                    nc.scalar.mul(out=terms[:, t, :], in_=h[:], mul=-0.1 / 6.0)
+                    nc.scalar.mul(out=plain[:, t, :], in_=h[:], mul=0.1 / 12.0)
             for g in range(G):
                 nc.scalar.activation(
-                    out=both[:, g, :], in_=both[:, g, :], func=ACT.Abs,
+                    out=reach[:, g, :], in_=reach[:, g, :], func=ACT.Abs,
                     bias=half_less_2_knots[:, g : g + 1], scale=1.0,
                 )
-            return both, terms
+            return reach, plain
 
-        def finish(k, bq, both, terms):
+        def finish(k, bq, reach, plain):
             cols = slice(bq * N_COLS, (bq + 1) * N_COLS)
             nc.vector.scalar_tensor_tensor(
-                out=terms[:, 0:G, :], in0=both[:], scalar=2.0, in1=terms[:, 0:G, :],
-                op0=ALU.subtract, op1=ALU.mult,
+                out=reach[:], in0=reach[:], scalar=2.0, in1=plain[:, 0:G, :],
+                op0=ALU.min, op1=ALU.mult,
             )
-            total = sums.tile([P, SUB, P], F32)
+            plain_sum = sums.tile([P, SUB, P], F32)
             for s in range(SUB):
                 for t in range(TERMS):
                     nc.tensor.matmul(
-                        out=total[:, s, :],
-                        lhsT=terms[:, t, s * P : (s + 1) * P],
+                        out=plain_sum[:, s, :],
+                        lhsT=plain[:, t, s * P : (s + 1) * P],
                         rhs=ident_f32[:],
                         is_transpose=True,
                         start=(t == 0),
                         stop=(t == TERMS - 1),
                     )
+            reach_sum = sums.tile([P, SUB, P], F32)
+            for s in range(SUB):
+                for g in range(G):
+                    nc.tensor.matmul(
+                        out=reach_sum[:, s, :],
+                        lhsT=reach[:, g, s * P : (s + 1) * P],
+                        rhs=ident_f32[:],
+                        is_transpose=True,
+                        start=(g == 0),
+                        stop=(g == G - 1),
+                    )
+            scaled = curves.tile([P, SUB, P], F32)
+            nc.scalar.mul(out=scaled[:], in_=plain_sum[:], mul=12.0)
             result = curves.tile([P, SUB, P], F32)
-            nc.scalar.mul(out=result[:], in_=total[:], mul=-6.0)
+            nc.vector.scalar_tensor_tensor(
+                out=result[:], in0=reach_sum[:], scalar=-6.0, in1=scaled[:],
+                op0=ALU.mult, op1=ALU.add,
+            )
             nc.sync.dma_start(
                 out=out[cols, k * P : (k + 1) * P].rearrange("(s p) i -> p s i", p=P),
                 in_=result[:],

@@ -142,7 +142,7 @@ def tile_advancedkanlayer_pa_kernel(
                     ident_bf16[:],
                 )
             x_cols = curves.tile([P, N_COLS], BF16)
-            nc.scalar.copy(out=x_cols[:], in_=x_turned[:])
+            nc.vector.tensor_copy(out=x_cols[:], in_=x_turned[:])
             folded = curves.tile([P, G, N_COLS], F32)
             for g in range(G):
                 nc.scalar.activation(
@@ -253,8 +253,8 @@ def tile_advancedkanlayer_pa_kernel(
         stage_b = {}
         for step in range(n_units + 2):
             if step < n_units:
-                prepare(*units[step])
                 stage_a[step] = fold(*units[step])
+                prepare(*units[step])
             if 0 <= step - 1 < n_units:
                 stage_b[step - 1] = products(*units[step - 1], *stage_a[step - 1])
             if 0 <= step - 2:

@@ -35,13 +35,24 @@ def tile_advancedkanlayer_pa_kernel(
         banks = ctx.enter_context(tc.psum_pool(name="banks", bufs=6))
         sums = ctx.enter_context(tc.psum_pool(name="sums", bufs=1))
 
+        x_rows = keep.tile([P, B // P, I], BF16)
+
+        def load_x(bq, first, last):
+            rows = slice(bq * N_COLS, (bq + 1) * N_COLS)
+            nc.sync.dma_start(
+                out=x_rows[:, bq * SUB : (bq + 1) * SUB, first:last],
+                in_=x_norm[rows, first:last].rearrange("(n p) i -> p n i", p=P),
+            )
+
+        load_x(0, 0, P)
+
         ident_bf16 = keep.tile([P, P], BF16)
         make_identity(nc, ident_bf16[:])
         ident_f32 = keep.tile([P, P], F32)
         make_identity(nc, ident_f32[:])
 
         knots_bf16 = keep.tile([P, G], BF16)
-        nc.sync.dma_start(out=knots_bf16[:], in_=grid_points.partition_broadcast(P))
+        nc.scalar.dma_start(out=knots_bf16[:], in_=grid_points.partition_broadcast(P))
         knots = keep.tile([P, G], F32)
         nc.vector.tensor_copy(out=knots[:], in_=knots_bf16[:])
         half_less_knots = keep.tile([P, G], F32)
@@ -59,15 +70,6 @@ def tile_advancedkanlayer_pa_kernel(
         g_scales = keep.tile([P, B], U8, align_bytes=64)
         w_codes = keep.tile([P, I_BLOCKS, TERMS, P], U32, align_bytes=64)
         w_scales = keep.tile([P, I_BLOCKS, TERMS, P], U8, align_bytes=64)
-
-        x_rows = keep.tile([P, B // P, I], BF16)
-
-        def load_x(bq):
-            rows = slice(bq * N_COLS, (bq + 1) * N_COLS)
-            nc.sync.dma_start(
-                out=x_rows[:, bq * SUB : (bq + 1) * SUB, :],
-                in_=x_norm[rows, :].rearrange("(n p) i -> p n i", p=P),
-            )
 
         def load_grad(bq):
             rows = slice(bq * N_COLS, (bq + 1) * N_COLS)
@@ -154,12 +156,12 @@ def tile_advancedkanlayer_pa_kernel(
 
         def products(k, bq, x_cols, folded):
             cols = slice(bq * N_COLS, (bq + 1) * N_COLS)
-            reach = curves.tile([P, G, N_COLS], F32)
+            reach = curves.tile([P, G, N_COLS], F32, bufs=3)
             nc.vector.scalar_tensor_tensor(
                 out=reach[:], in0=x_cols[:].unsqueeze(1).to_broadcast([P, G, N_COLS]),
                 scalar=2.0, in1=folded[:], op0=ALU.mult, op1=ALU.subtract,
             )
-            plain = curves.tile([P, TERMS, N_COLS], F32)
+            plain = curves.tile([P, TERMS, N_COLS], F32, bufs=3)
             for t in range(TERMS):
                 h = banks.tile([P, N_COLS], F32, tag="bank")
                 nc.tensor.matmul_mx(
@@ -185,12 +187,7 @@ def tile_advancedkanlayer_pa_kernel(
                 )
             return reach, plain
 
-        def finish(k, bq, reach, plain):
-            cols = slice(bq * N_COLS, (bq + 1) * N_COLS)
-            nc.vector.scalar_tensor_tensor(
-                out=reach[:], in0=reach[:], scalar=2.0, in1=plain[:, 0:G, :],
-                op0=ALU.min, op1=ALU.mult,
-            )
+        def finish(k, bq, reach, plain, pieces):
             plain_sum = sums.tile([P, SUB, P], F32)
             for s in range(SUB):
                 for t in range(TERMS):
@@ -202,28 +199,40 @@ def tile_advancedkanlayer_pa_kernel(
                         start=(t == 0),
                         stop=(t == TERMS - 1),
                     )
-            reach_sum = sums.tile([P, SUB, P], F32)
-            for s in range(SUB):
-                for g in range(G):
-                    nc.tensor.matmul(
-                        out=reach_sum[:, s, :],
-                        lhsT=reach[:, g, s * P : (s + 1) * P],
-                        rhs=ident_f32[:],
-                        is_transpose=True,
-                        start=(g == 0),
-                        stop=(g == G - 1),
-                    )
             scaled = curves.tile([P, SUB, P], F32)
             nc.scalar.mul(out=scaled[:], in_=plain_sum[:], mul=12.0)
             result = curves.tile([P, SUB, P], F32)
-            nc.vector.scalar_tensor_tensor(
-                out=result[:], in0=reach_sum[:], scalar=-6.0, in1=scaled[:],
-                op0=ALU.mult, op1=ALU.add,
-            )
-            nc.sync.dma_start(
-                out=out[cols, k * P : (k + 1) * P].rearrange("(s p) i -> p s i", p=P),
-                in_=result[:],
-            )
+            per_piece = SUB // pieces
+            for piece in range(pieces):
+                if pieces == 1:
+                    reach_sum = sums.tile([P, per_piece, P], F32)
+                else:
+                    reach_sum = banks.tile([P, per_piece, P], F32, tag="bank")
+                subs = slice(piece * per_piece, (piece + 1) * per_piece)
+                inner = slice(piece * per_piece * P, (piece + 1) * per_piece * P)
+                nc.vector.scalar_tensor_tensor(
+                    out=reach[:, :, inner], in0=reach[:, :, inner], scalar=2.0,
+                    in1=plain[:, 0:G, inner], op0=ALU.min, op1=ALU.mult,
+                )
+                for s in range(piece * per_piece, (piece + 1) * per_piece):
+                    for g in range(G):
+                        nc.tensor.matmul(
+                            out=reach_sum[:, s - piece * per_piece, :],
+                            lhsT=reach[:, g, s * P : (s + 1) * P],
+                            rhs=ident_f32[:],
+                            is_transpose=True,
+                            start=(g == 0),
+                            stop=(g == G - 1),
+                        )
+                nc.vector.scalar_tensor_tensor(
+                    out=result[:, subs, :], in0=reach_sum[:], scalar=-6.0,
+                    in1=scaled[:, subs, :], op0=ALU.mult, op1=ALU.add,
+                )
+                rows = slice(bq * N_COLS + piece * per_piece * P, bq * N_COLS + (piece + 1) * per_piece * P)
+                nc.sync.dma_start(
+                    out=out[rows, k * P : (k + 1) * P].rearrange("(s p) i -> p s i", p=P),
+                    in_=result[:, subs, :],
+                )
 
         units = [(k, bq) for k in range(I_BLOCKS) for bq in range(B_BLOCKS)]
 
@@ -241,11 +250,12 @@ def tile_advancedkanlayer_pa_kernel(
                     w_loaded[k + 2] = load_weights(k + 2)
 
         g_loaded[0] = load_grad(0)
-        load_x(0)
         w_loaded[0] = load_weights(0)
+        load_x(1, 0, I)
         g_loaded[1] = load_grad(1)
-        for bq in range(1, B_BLOCKS):
-            load_x(bq)
+        load_x(0, P, I)
+        for bq in range(2, B_BLOCKS):
+            load_x(bq, 0, I)
         w_loaded[1] = load_weights(1)
 
         n_units = len(units)
@@ -258,4 +268,4 @@ def tile_advancedkanlayer_pa_kernel(
             if 0 <= step - 1 < n_units:
                 stage_b[step - 1] = products(*units[step - 1], *stage_a[step - 1])
             if 0 <= step - 2:
-                finish(*units[step - 2], *stage_b[step - 2])
+                finish(*units[step - 2], *stage_b[step - 2], SUB if step - 2 == n_units - 1 else 1)

@@ -20,6 +20,8 @@ I_BLOCKS = I // P
 B_BLOCKS = B // N_COLS
 SUB = N_COLS // P
 TERMS = G + 1
+POOL_KNOTS = 4
+H_BANKS = 6
 
 FLOPS = 2 * B * O * (I * G + I)
 
@@ -32,7 +34,7 @@ def tile_advancedkanlayer_pa_kernel(
         keep = ctx.enter_context(tc.tile_pool(name="keep", bufs=1))
         stage = ctx.enter_context(tc.tile_pool(name="stage", bufs=1))
         curves = ctx.enter_context(tc.tile_pool(name="curves", bufs=2))
-        banks = ctx.enter_context(tc.psum_pool(name="banks", bufs=6))
+        banks = ctx.enter_context(tc.psum_pool(name="banks", bufs=H_BANKS))
         sums = ctx.enter_context(tc.psum_pool(name="sums", bufs=1))
 
         x_rows = keep.tile([P, B // P, I], BF16)
@@ -73,7 +75,7 @@ def tile_advancedkanlayer_pa_kernel(
 
         def load_grad(bq):
             rows = slice(bq * N_COLS, (bq + 1) * N_COLS)
-            g_rows = stage.tile([P, SUB, O], BF16, bufs=2)
+            g_rows = stage.tile([P, SUB, O], BF16, bufs=B_BLOCKS)
             nc.sync.dma_start(
                 out=g_rows[:], in_=grad_out[rows, :].rearrange("(n p) o -> p n o", p=P)
             )
@@ -135,7 +137,11 @@ def tile_advancedkanlayer_pa_kernel(
                 in_=w_grouped[:, G, :, :].rearrange("p i j -> p (i j)"),
             )
 
-        def fold(k, bq):
+        units = [(k, bq) for k in range(I_BLOCKS) for bq in range(B_BLOCKS)]
+        n_units = len(units)
+
+        def turn_x(u):
+            k, bq = units[u]
             x_turned = banks.tile([P, N_COLS], BF16, tag="bank")
             for n in range(SUB):
                 nc.tensor.transpose(
@@ -143,129 +149,165 @@ def tile_advancedkanlayer_pa_kernel(
                     x_rows[:, bq * SUB + n, k * P : (k + 1) * P],
                     ident_bf16[:],
                 )
-            x_cols = curves.tile([P, N_COLS], BF16)
-            nc.vector.tensor_copy(out=x_cols[:], in_=x_turned[:])
-            folded = curves.tile([P, G, N_COLS], F32)
+            return x_turned
+
+        def copy_x(x_turned):
+            x_twice = curves.tile([P, N_COLS], BF16, bufs=4)
+            nc.vector.tensor_scalar_mul(out=x_twice[:], in0=x_turned[:], scalar1=2.0)
+            return x_twice
+
+        def fold(x_twice):
+            folded = curves.tile([P, G, N_COLS], F32, bufs=4)
             for g in range(G):
                 nc.scalar.activation(
-                    out=folded[:, g, :], in_=x_cols[:], func=ACT.Abs,
-                    bias=half_less_knots[:, g : g + 1], scale=1.0,
+                    out=folded[:, g, :], in_=x_twice[:], func=ACT.Abs,
+                    bias=half_less_knots[:, g : g + 1], scale=0.5,
                 )
             nc.scalar.activation(out=folded[:], in_=folded[:], func=ACT.Abs, bias=-1.0, scale=1.0)
-            return x_cols, folded
+            return folded
 
-        def products(k, bq, x_cols, folded):
+        def mx_product(u, t):
+            k, bq = units[u]
             cols = slice(bq * N_COLS, (bq + 1) * N_COLS)
-            reach = curves.tile([P, G, N_COLS], F32, bufs=3)
-            nc.vector.scalar_tensor_tensor(
-                out=reach[:], in0=x_cols[:].unsqueeze(1).to_broadcast([P, G, N_COLS]),
-                scalar=2.0, in1=folded[:], op0=ALU.mult, op1=ALU.subtract,
+            h = banks.tile([P, N_COLS], F32, tag="bank")
+            nc.tensor.matmul_mx(
+                out=h[:],
+                lhsT=w_codes[:, k, t, :].bitcast(E4M3_X4),
+                lhsT_scale=w_scales[:, k, t, :],
+                rhs=g_codes[:, cols].bitcast(E5M2_X4),
+                rhs_scale=g_scales[:, cols],
+                start=True,
+                stop=True,
             )
-            plain = curves.tile([P, TERMS, N_COLS], F32, bufs=3)
-            for t in range(TERMS):
-                h = banks.tile([P, N_COLS], F32, tag="bank")
-                nc.tensor.matmul_mx(
-                    out=h[:],
-                    lhsT=w_codes[:, k, t, :].bitcast(E4M3_X4),
-                    lhsT_scale=w_scales[:, k, t, :],
-                    rhs=g_codes[:, cols].bitcast(E5M2_X4),
-                    rhs_scale=g_scales[:, cols],
-                    start=True,
-                    stop=True,
-                )
-                if t < G:
-                    nc.vector.scalar_tensor_tensor(
-                        out=plain[:, t, :], in0=folded[:, t, :], scalar=0.5, in1=h[:],
-                        op0=ALU.subtract, op1=ALU.mult,
-                    )
-                else:
-                    nc.scalar.mul(out=plain[:, t, :], in_=h[:], mul=0.1 / 12.0)
-            for g in range(G):
-                nc.scalar.activation(
-                    out=reach[:, g, :], in_=reach[:, g, :], func=ACT.Abs,
-                    bias=half_less_2_knots[:, g : g + 1], scale=1.0,
-                )
-            return reach, plain
+            return h
 
-        def finish(k, bq, reach, plain, pieces):
-            plain_sum = sums.tile([P, SUB, P], F32)
-            for s in range(SUB):
-                for t in range(TERMS):
+        def sum_terms(target, tiles, n_terms, first_sub, n_subs):
+            for s in range(n_subs):
+                b0 = (first_sub + s) * P
+                for t in range(n_terms):
                     nc.tensor.matmul(
-                        out=plain_sum[:, s, :],
-                        lhsT=plain[:, t, s * P : (s + 1) * P],
+                        out=target[:, s, :],
+                        lhsT=tiles[:, t, b0 : b0 + P],
                         rhs=ident_f32[:],
                         is_transpose=True,
                         start=(t == 0),
-                        stop=(t == TERMS - 1),
+                        stop=(t == n_terms - 1),
                     )
-            scaled = curves.tile([P, SUB, P], F32)
-            nc.scalar.mul(out=scaled[:], in_=plain_sum[:], mul=12.0)
-            result = curves.tile([P, SUB, P], F32)
-            per_piece = SUB // pieces
-            for piece in range(pieces):
-                if pieces == 1:
-                    reach_sum = sums.tile([P, per_piece, P], F32)
-                else:
-                    reach_sum = banks.tile([P, per_piece, P], F32, tag="bank")
-                subs = slice(piece * per_piece, (piece + 1) * per_piece)
-                inner = slice(piece * per_piece * P, (piece + 1) * per_piece * P)
-                nc.vector.scalar_tensor_tensor(
-                    out=reach[:, :, inner], in0=reach[:, :, inner], scalar=2.0,
-                    in1=plain[:, 0:G, inner], op0=ALU.min, op1=ALU.mult,
-                )
-                for s in range(piece * per_piece, (piece + 1) * per_piece):
-                    for g in range(G):
-                        nc.tensor.matmul(
-                            out=reach_sum[:, s - piece * per_piece, :],
-                            lhsT=reach[:, g, s * P : (s + 1) * P],
-                            rhs=ident_f32[:],
-                            is_transpose=True,
-                            start=(g == 0),
-                            stop=(g == G - 1),
-                        )
-                nc.vector.scalar_tensor_tensor(
-                    out=result[:, subs, :], in0=reach_sum[:], scalar=-6.0,
-                    in1=scaled[:, subs, :], op0=ALU.mult, op1=ALU.add,
-                )
-                rows = slice(bq * N_COLS + piece * per_piece * P, bq * N_COLS + (piece + 1) * per_piece * P)
-                nc.sync.dma_start(
-                    out=out[rows, k * P : (k + 1) * P].rearrange("(s p) i -> p s i", p=P),
-                    in_=result[:, subs, :],
-                )
 
-        units = [(k, bq) for k in range(I_BLOCKS) for bq in range(B_BLOCKS)]
+        def last_product(folded, plain, first, last):
+            nc.vector.scalar_tensor_tensor(
+                out=folded[:, :, first:last], in0=folded[:, :, first:last], scalar=2.0,
+                in1=plain[:, 0:G, first:last], op0=ALU.min, op1=ALU.mult,
+            )
+
+        def join(u, reach_sum, scaled, result, first_sub, n_subs):
+            k, bq = units[u]
+            subs = slice(first_sub, first_sub + n_subs)
+            nc.vector.scalar_tensor_tensor(
+                out=result[:, subs, :], in0=reach_sum[:], scalar=-6.0,
+                in1=scaled[:, subs, :], op0=ALU.mult, op1=ALU.add,
+            )
+            rows = slice(bq * N_COLS + first_sub * P, bq * N_COLS + (first_sub + n_subs) * P)
+            nc.sync.dma_start(
+                out=out[rows, k * P : (k + 1) * P].rearrange("(s p) i -> p s i", p=P),
+                in_=result[:, subs, :],
+            )
 
         g_loaded = {}
         w_loaded = {}
-
-        def prepare(k, bq):
-            if k == 0:
-                quantise_grad(bq, g_loaded[bq])
-                if bq + 2 < B_BLOCKS:
-                    g_loaded[bq + 2] = load_grad(bq + 2)
-            if bq == 0:
-                quantise_weights(k, w_loaded[k])
-                if k + 2 < I_BLOCKS:
-                    w_loaded[k + 2] = load_weights(k + 2)
-
         g_loaded[0] = load_grad(0)
         w_loaded[0] = load_weights(0)
         load_x(1, 0, I)
         g_loaded[1] = load_grad(1)
+        load_x(2, 0, I)
+        g_loaded[2] = load_grad(2)
+        load_x(3, 0, I)
+        g_loaded[3] = load_grad(3)
         load_x(0, P, I)
-        for bq in range(2, B_BLOCKS):
-            load_x(bq, 0, I)
         w_loaded[1] = load_weights(1)
 
-        n_units = len(units)
-        stage_a = {}
-        stage_b = {}
-        for step in range(n_units + 2):
-            if step < n_units:
-                stage_a[step] = fold(*units[step])
-                prepare(*units[step])
-            if 0 <= step - 1 < n_units:
-                stage_b[step - 1] = products(*units[step - 1], *stage_a[step - 1])
-            if 0 <= step - 2:
-                finish(*units[step - 2], *stage_b[step - 2], SUB if step - 2 == n_units - 1 else 1)
+        x_banks = {}
+        x_twices = {}
+        foldeds = {}
+        plains = {}
+        hs = {}
+        scaleds = {}
+        results = {}
+
+        with tc.manual_schedule(engines={mybir.EngineType.DVE, mybir.EngineType.Pool}):
+            for t in range(-2, n_units + 2):
+                last_unit = n_units - 1
+                if 0 <= t - 1 < n_units:
+                    folded = foldeds[t - 1]
+                    for g in range(G):
+                        nc.scalar.activation(
+                            out=folded[:, g, :], in_=folded[:, g, :], func=ACT.Abs,
+                            bias=half_less_2_knots[:, g : g + 1], scale=1.0,
+                        )
+                if 0 <= t - 2 < last_unit:
+                    reach_sum = sums.tile([P, SUB, P], F32)
+                    sum_terms(reach_sum, foldeds[t - 2], G, 0, SUB)
+                if 0 <= t < n_units:
+                    folded = foldeds[t]
+                    plain = curves.tile([P, TERMS, N_COLS], F32, bufs=2)
+                    plains[t] = plain
+                    for g in range(G):
+                        nc.vector.scalar_tensor_tensor(
+                            out=plain[:, g, :], in0=folded[:, g, :], scalar=0.5, in1=hs[t, g][:],
+                            op0=ALU.subtract, op1=ALU.mult,
+                        )
+                        if g < POOL_KNOTS:
+                            nc.gpsimd.tensor_tensor(
+                                out=folded[:, g, :], in0=x_twices[t][:], in1=folded[:, g, :],
+                                op=ALU.subtract,
+                            )
+                        if g + H_BANKS < TERMS:
+                            hs[t, g + H_BANKS] = mx_product(t, g + H_BANKS)
+                        if g == TERMS - H_BANKS and t + 2 < n_units:
+                            x_banks[t + 2] = turn_x(t + 2)
+                    nc.vector.tensor_scalar_mul(
+                        out=plain[:, G, :], in0=hs[t, G][:], scalar1=0.1 / 12.0
+                    )
+                elif t + 2 < n_units:
+                    x_banks[t + 2] = turn_x(t + 2)
+                if 0 <= t - 2 < last_unit:
+                    results[t - 2] = curves.tile([P, SUB, P], F32, name="result")
+                    join(t - 2, reach_sum, scaleds[t - 2], results[t - 2], 0, SUB)
+                if t + 2 < n_units:
+                    x_twices[t + 2] = copy_x(x_banks[t + 2])
+                if 0 <= t < n_units:
+                    nc.vector.tensor_tensor(
+                        out=folded[:, POOL_KNOTS:G, :],
+                        in0=x_twices[t][:].unsqueeze(1).to_broadcast([P, G - POOL_KNOTS, N_COLS]),
+                        in1=folded[:, POOL_KNOTS:G, :],
+                        op=ALU.subtract,
+                    )
+                    plain_sum = sums.tile([P, SUB, P], F32)
+                    sum_terms(plain_sum, plain, TERMS, 0, SUB)
+                    scaleds[t] = curves.tile([P, SUB, P], F32, name="scaled")
+                    nc.scalar.mul(out=scaleds[t][:], in_=plain_sum[:], mul=12.0)
+                if 0 <= t - 1 < last_unit:
+                    last_product(foldeds[t - 1], plains[t - 1], 0, N_COLS)
+                if t - 1 == last_unit:
+                    results[last_unit] = curves.tile([P, SUB, P], F32, name="result")
+                    for s in range(SUB):
+                        last_product(foldeds[last_unit], plains[last_unit], s * P, (s + 1) * P)
+                        piece_sum = banks.tile([P, 1, P], F32, tag="bank")
+                        sum_terms(piece_sum, foldeds[last_unit], G, s, 1)
+                        join(last_unit, piece_sum, scaleds[last_unit], results[last_unit], s, 1)
+                if t == -2:
+                    quantise_grad(0, g_loaded[0])
+                    quantise_weights(0, w_loaded[0])
+                    w_loaded[2] = load_weights(2)
+                if t == -1:
+                    for bq in range(1, B_BLOCKS):
+                        quantise_grad(bq, g_loaded[bq])
+                if t >= 0 and (t + 2) % B_BLOCKS == 0 and t + 2 < n_units:
+                    k = (t + 2) // B_BLOCKS
+                    quantise_weights(k, w_loaded[k])
+                    if k + 2 < I_BLOCKS:
+                        w_loaded[k + 2] = load_weights(k + 2)
+                if 0 <= t + 1 < n_units:
+                    for term in range(H_BANKS):
+                        hs[t + 1, term] = mx_product(t + 1, term)
+                    foldeds[t + 1] = fold(x_twices[t + 1])

@@ -21,6 +21,7 @@ B_BLOCKS = B // N_COLS
 SUB = N_COLS // P
 TERMS = G + 1
 POOL_KNOTS = 4
+POOL_RUN = 2
 H_BANKS = 6
 
 FLOPS = 2 * B * O * (I * G + I)
@@ -256,15 +257,20 @@ def tile_advancedkanlayer_pa_kernel(
                             out=plain[:, g, :], in0=folded[:, g, :], scalar=0.5, in1=hs[t, g][:],
                             op0=ALU.subtract, op1=ALU.mult,
                         )
-                        if g < POOL_KNOTS:
+                        if g < POOL_KNOTS and (g + 1) % POOL_RUN == 0:
+                            run = slice(g + 1 - POOL_RUN, g + 1)
                             nc.gpsimd.tensor_tensor(
-                                out=folded[:, g, :], in0=x_twices[t][:], in1=folded[:, g, :],
+                                out=folded[:, run, :],
+                                in0=x_twices[t][:].unsqueeze(1).to_broadcast([P, POOL_RUN, N_COLS]),
+                                in1=folded[:, run, :],
                                 op=ALU.subtract,
                             )
                         if g + H_BANKS < TERMS:
                             hs[t, g + H_BANKS] = mx_product(t, g + H_BANKS)
                         if g == TERMS - H_BANKS and t + 2 < n_units:
                             x_banks[t + 2] = turn_x(t + 2)
+                        if g == TERMS - H_BANKS + 1:
+                            x_again = turn_x(t)
                     nc.vector.tensor_scalar_mul(
                         out=plain[:, G, :], in0=hs[t, G][:], scalar1=0.1 / 12.0
                     )
@@ -276,11 +282,13 @@ def tile_advancedkanlayer_pa_kernel(
                 if t + 2 < n_units:
                     x_twices[t + 2] = copy_x(x_banks[t + 2])
                 if 0 <= t < n_units:
-                    nc.vector.tensor_tensor(
+                    nc.vector.scalar_tensor_tensor(
                         out=folded[:, POOL_KNOTS:G, :],
-                        in0=x_twices[t][:].unsqueeze(1).to_broadcast([P, G - POOL_KNOTS, N_COLS]),
+                        in0=x_again[:].unsqueeze(1).to_broadcast([P, G - POOL_KNOTS, N_COLS]),
+                        scalar=2.0,
                         in1=folded[:, POOL_KNOTS:G, :],
-                        op=ALU.subtract,
+                        op0=ALU.mult,
+                        op1=ALU.subtract,
                     )
                     plain_sum = sums.tile([P, SUB, P], F32)
                     sum_terms(plain_sum, plain, TERMS, 0, SUB)
@@ -290,11 +298,18 @@ def tile_advancedkanlayer_pa_kernel(
                     last_product(foldeds[t - 1], plains[t - 1], 0, N_COLS)
                 if t - 1 == last_unit:
                     results[last_unit] = curves.tile([P, SUB, P], F32, name="result")
-                    for s in range(SUB):
-                        last_product(foldeds[last_unit], plains[last_unit], s * P, (s + 1) * P)
-                        piece_sum = banks.tile([P, 1, P], F32, tag="bank")
-                        sum_terms(piece_sum, foldeds[last_unit], G, s, 1)
-                        join(last_unit, piece_sum, scaleds[last_unit], results[last_unit], s, 1)
+                    piece_sums = {}
+                    for s in range(SUB + 1):
+                        if s < SUB:
+                            last_product(foldeds[last_unit], plains[last_unit], s * P, (s + 1) * P)
+                            piece_sum = banks.tile([P, 1, P], F32, tag="bank")
+                            sum_terms(piece_sum, foldeds[last_unit], G, s, 1)
+                            piece_sums[s] = piece_sum
+                        if s >= 1:
+                            join(
+                                last_unit, piece_sums[s - 1], scaleds[last_unit],
+                                results[last_unit], s - 1, 1,
+                            )
                 if t == -2:
                     quantise_grad(0, g_loaded[0])
                     quantise_weights(0, w_loaded[0])

@@ -235,7 +235,7 @@ def tile_advancedkanlayer_pa_kernel(
         scaleds = {}
         results = {}
 
-        with tc.manual_schedule(engines={mybir.EngineType.DVE, mybir.EngineType.Pool}):
+        with tc.manual_schedule(engines={mybir.EngineType.Pool}):
             for t in range(-2, n_units + 2):
                 last_unit = n_units - 1
                 if 0 <= t - 1 < n_units:

@@ -235,7 +235,7 @@ def tile_advancedkanlayer_pa_kernel(
         scaleds = {}
         results = {}
 
-        with tc.manual_schedule(engines={mybir.EngineType.Pool}):
+        with tc.manual_schedule(engines={mybir.EngineType.PE, mybir.EngineType.Pool}):
             for t in range(-2, n_units + 2):
                 last_unit = n_units - 1
                 if 0 <= t - 1 < n_units:
@@ -245,9 +245,6 @@ def tile_advancedkanlayer_pa_kernel(
                             out=folded[:, g, :], in_=folded[:, g, :], func=ACT.Abs,
                             bias=half_less_2_knots[:, g : g + 1], scale=1.0,
                         )
-                if 0 <= t - 2 < last_unit:
-                    reach_sum = sums.tile([P, SUB, P], F32)
-                    sum_terms(reach_sum, foldeds[t - 2], G, 0, SUB)
                 if 0 <= t < n_units:
                     folded = foldeds[t]
                     plain = curves.tile([P, TERMS, N_COLS], F32, bufs=2)
@@ -267,14 +264,13 @@ def tile_advancedkanlayer_pa_kernel(
                             )
                         if g + H_BANKS < TERMS:
                             hs[t, g + H_BANKS] = mx_product(t, g + H_BANKS)
-                        if g == TERMS - H_BANKS and t + 2 < n_units:
-                            x_banks[t + 2] = turn_x(t + 2)
-                        if g == TERMS - H_BANKS + 1:
-                            x_again = turn_x(t)
                     nc.vector.tensor_scalar_mul(
                         out=plain[:, G, :], in0=hs[t, G][:], scalar1=0.1 / 12.0
                     )
-                elif t + 2 < n_units:
+                if 0 <= t - 2 < last_unit:
+                    reach_sum = sums.tile([P, SUB, P], F32)
+                    sum_terms(reach_sum, foldeds[t - 2], G, 0, SUB)
+                if t + 2 < n_units:
                     x_banks[t + 2] = turn_x(t + 2)
                 if 0 <= t - 2 < last_unit:
                     results[t - 2] = curves.tile([P, SUB, P], F32, name="result")
@@ -282,13 +278,11 @@ def tile_advancedkanlayer_pa_kernel(
                 if t + 2 < n_units:
                     x_twices[t + 2] = copy_x(x_banks[t + 2])
                 if 0 <= t < n_units:
-                    nc.vector.scalar_tensor_tensor(
+                    nc.vector.tensor_tensor(
                         out=folded[:, POOL_KNOTS:G, :],
-                        in0=x_again[:].unsqueeze(1).to_broadcast([P, G - POOL_KNOTS, N_COLS]),
-                        scalar=2.0,
+                        in0=x_twices[t][:].unsqueeze(1).to_broadcast([P, G - POOL_KNOTS, N_COLS]),
                         in1=folded[:, POOL_KNOTS:G, :],
-                        op0=ALU.mult,
-                        op1=ALU.subtract,
+                        op=ALU.subtract,
                     )
                     plain_sum = sums.tile([P, SUB, P], F32)
                     sum_terms(plain_sum, plain, TERMS, 0, SUB)

@@ -20,8 +20,8 @@ I_BLOCKS = I // P
 B_BLOCKS = B // N_COLS
 SUB = N_COLS // P
 TERMS = G + 1
-POOL_KNOTS = 4
-POOL_RUN = 2
+POOL_RUNS = (1, 2)
+POOL_KNOTS = sum(POOL_RUNS)
 H_BANKS = 6
 
 FLOPS = 2 * B * O * (I * G + I)
@@ -227,6 +227,7 @@ def tile_advancedkanlayer_pa_kernel(
         load_x(0, P, I)
         w_loaded[1] = load_weights(1)
 
+        run_ends = {sum(POOL_RUNS[: j + 1]): POOL_RUNS[j] for j in range(len(POOL_RUNS))}
         x_banks = {}
         x_twices = {}
         foldeds = {}
@@ -254,11 +255,13 @@ def tile_advancedkanlayer_pa_kernel(
                             out=plain[:, g, :], in0=folded[:, g, :], scalar=0.5, in1=hs[t, g][:],
                             op0=ALU.subtract, op1=ALU.mult,
                         )
-                        if g < POOL_KNOTS and (g + 1) % POOL_RUN == 0:
-                            run = slice(g + 1 - POOL_RUN, g + 1)
+                        if g + 1 in run_ends:
+                            run = slice(g + 1 - run_ends[g + 1], g + 1)
                             nc.gpsimd.tensor_tensor(
                                 out=folded[:, run, :],
-                                in0=x_twices[t][:].unsqueeze(1).to_broadcast([P, POOL_RUN, N_COLS]),
+                                in0=x_twices[t][:].unsqueeze(1).to_broadcast(
+                                    [P, run_ends[g + 1], N_COLS]
+                                ),
                                 in1=folded[:, run, :],
                                 op=ALU.subtract,
                             )

from contextlib import ExitStack

import concourse.mybir as mybir
from concourse.masks import make_identity

F32 = mybir.dt.float32
BF16 = mybir.dt.bfloat16
U32 = mybir.dt.uint32
U8 = mybir.dt.uint8
E4M3_X4 = mybir.dt.float8_e4m3fn_x4
E5M2_X4 = mybir.dt.float8_e5m2_x4
ALU = mybir.AluOpType
ACT = mybir.ActivationFunctionType

B, I, O, G = 2048, 512, 512, 8
P = 128
PACK = 4
N_COLS = 512
I_BLOCKS = I // P
B_BLOCKS = B // N_COLS
SUB = N_COLS // P
TERMS = G + 1
POOL_RUNS = (1, 2)
POOL_KNOTS = sum(POOL_RUNS)
H_BANKS = 6

FLOPS = 2 * B * O * (I * G + I)


def tile_advancedkanlayer_pa_kernel(
    tc, x_norm, spline_weight, base_activation, grid_points, grad_out, out
):
    nc = tc.nc
    with ExitStack() as ctx:
        keep = ctx.enter_context(tc.tile_pool(name="keep", bufs=1))
        stage = ctx.enter_context(tc.tile_pool(name="stage", bufs=1))
        curves = ctx.enter_context(tc.tile_pool(name="curves", bufs=2))
        banks = ctx.enter_context(tc.psum_pool(name="banks", bufs=H_BANKS))
        sums = ctx.enter_context(tc.psum_pool(name="sums", bufs=1))

        x_rows = keep.tile([P, B // P, I], BF16)

        def load_x(bq, first, last):
            rows = slice(bq * N_COLS, (bq + 1) * N_COLS)
            nc.sync.dma_start(
                out=x_rows[:, bq * SUB : (bq + 1) * SUB, first:last],
                in_=x_norm[rows, first:last].rearrange("(n p) i -> p n i", p=P),
            )

        load_x(0, 0, P)

        ident_bf16 = keep.tile([P, P], BF16)
        make_identity(nc, ident_bf16[:])
        ident_f32 = keep.tile([P, P], F32)
        make_identity(nc, ident_f32[:])

        knots_bf16 = keep.tile([P, G], BF16)
        nc.scalar.dma_start(out=knots_bf16[:], in_=grid_points.partition_broadcast(P))
        knots = keep.tile([P, G], F32)
        nc.vector.tensor_copy(out=knots[:], in_=knots_bf16[:])
        half_less_knots = keep.tile([P, G], F32)
        nc.vector.tensor_scalar(
            out=half_less_knots[:], in0=knots[:], scalar1=-1.0, scalar2=0.5,
            op0=ALU.mult, op1=ALU.add,
        )
        half_less_2_knots = keep.tile([P, G], F32)
        nc.vector.tensor_scalar(
            out=half_less_2_knots[:], in0=knots[:], scalar1=-2.0, scalar2=0.5,
            op0=ALU.mult, op1=ALU.add,
        )

        g_codes = keep.tile([P, B], U32, align_bytes=64)
        g_scales = keep.tile([P, B], U8, align_bytes=64)
        w_codes = keep.tile([P, I_BLOCKS, TERMS, P], U32, align_bytes=64)
        w_scales = keep.tile([P, I_BLOCKS, TERMS, P], U8, align_bytes=64)

        def load_grad(bq):
            rows = slice(bq * N_COLS, (bq + 1) * N_COLS)
            g_rows = stage.tile([P, SUB, O], BF16, bufs=B_BLOCKS)
            nc.sync.dma_start(
                out=g_rows[:], in_=grad_out[rows, :].rearrange("(n p) o -> p n o", p=P)
            )
            return g_rows

        def quantise_grad(bq, g_rows):
            g_grouped = stage.tile([P, N_COLS * PACK], BF16, align_bytes=64)
            g_pairs = g_grouped[:].bitcast(F32).rearrange("p (n b u) -> p n b u", n=SUB, u=2)
            for half in range(SUB // 2):
                turned = banks.tile([P, 2, 2, P], F32, tag="bank")
                for m in range(2):
                    words = g_rows[:, 2 * half + m, :].bitcast(F32)
                    words = words.rearrange("b (p u) -> b u p", u=2)
                    for u in range(2):
                        nc.tensor.transpose(turned[:, m, u, :], words[:, u, :], ident_f32[:])
                nc.vector.tensor_copy(
                    out=g_pairs[:, 2 * half : 2 * half + 2, :, :],
                    in_=turned[:].rearrange("p m u b -> p m b u"),
                )
            cols = slice(bq * N_COLS, (bq + 1) * N_COLS)
            nc.vector.quantize_mx(
                out=g_codes[:, cols].bitcast(E5M2_X4), scales=g_scales[:, cols], in_=g_grouped[:]
            )

        def load_weights(k):
            w_rows = stage.tile([P, PACK, TERMS * P], BF16, bufs=2)
            nc.sync.dma_start(
                out=w_rows[:, :, 0 : G * P],
                in_=spline_weight.rearrange("(p j) i g -> p j (i g)", j=PACK)[
                    :, :, k * G * P : (k + 1) * G * P
                ],
            )
            nc.sync.dma_start(
                out=w_rows[:, :, G * P : TERMS * P],
                in_=base_activation.rearrange("(p j) i -> p j i", j=PACK)[
                    :, :, k * P : (k + 1) * P
                ],
            )
            return w_rows

        def quantise_weights(k, w_rows):
            w_grouped = stage.tile([P, TERMS, P, PACK], BF16, align_bytes=64)
            nc.vector.tensor_copy(
                out=w_grouped[:, 0:G, :, :],
                in_=w_rows[:, :, 0 : G * P].rearrange("p j (i g) -> p g i j", g=G),
            )
            nc.vector.tensor_copy(
                out=w_grouped[:, G, :, :],
                in_=w_rows[:, :, G * P : TERMS * P].rearrange("p j i -> p i j"),
            )
            nc.vector.quantize_mx(
                out=w_codes[:, k, 0:G, :].rearrange("p g i -> p (g i)").bitcast(E4M3_X4),
                scales=w_scales[:, k, 0:G, :].rearrange("p g i -> p (g i)"),
                in_=w_grouped[:, 0:G, :, :].rearrange("p g i j -> p (g i j)"),
            )
            nc.vector.quantize_mx(
                out=w_codes[:, k, G, :].bitcast(E4M3_X4),
                scales=w_scales[:, k, G, :],
                in_=w_grouped[:, G, :, :].rearrange("p i j -> p (i j)"),
            )

        units = [(k, bq) for k in range(I_BLOCKS) for bq in range(B_BLOCKS)]
        n_units = len(units)

        def turn_x(u):
            k, bq = units[u]
            x_turned = banks.tile([P, N_COLS], BF16, tag="bank")
            for n in range(SUB):
                nc.tensor.transpose(
                    x_turned[:, n * P : (n + 1) * P],
                    x_rows[:, bq * SUB + n, k * P : (k + 1) * P],
                    ident_bf16[:],
                )
            return x_turned

        def copy_x(x_turned):
            x_twice = curves.tile([P, N_COLS], BF16, bufs=4)
            nc.vector.tensor_scalar_mul(out=x_twice[:], in0=x_turned[:], scalar1=2.0)
            return x_twice

        def fold(x_twice):
            folded = curves.tile([P, G, N_COLS], F32, bufs=4)
            for g in range(G):
                nc.scalar.activation(
                    out=folded[:, g, :], in_=x_twice[:], func=ACT.Abs,
                    bias=half_less_knots[:, g : g + 1], scale=0.5,
                )
            nc.scalar.activation(out=folded[:], in_=folded[:], func=ACT.Abs, bias=-1.0, scale=1.0)
            return folded

        def mx_product(u, t):
            k, bq = units[u]
            cols = slice(bq * N_COLS, (bq + 1) * N_COLS)
            h = banks.tile([P, N_COLS], F32, tag="bank")
            nc.tensor.matmul_mx(
                out=h[:],
                lhsT=w_codes[:, k, t, :].bitcast(E4M3_X4),
                lhsT_scale=w_scales[:, k, t, :],
                rhs=g_codes[:, cols].bitcast(E5M2_X4),
                rhs_scale=g_scales[:, cols],
                start=True,
                stop=True,
            )
            return h

        def sum_terms(target, tiles, n_terms, first_sub, n_subs):
            for s in range(n_subs):
                b0 = (first_sub + s) * P
                for t in range(n_terms):
                    nc.tensor.matmul(
                        out=target[:, s, :],
                        lhsT=tiles[:, t, b0 : b0 + P],
                        rhs=ident_f32[:],
                        is_transpose=True,
                        start=(t == 0),
                        stop=(t == n_terms - 1),
                    )

        def last_product(folded, plain, first, last):
            nc.vector.scalar_tensor_tensor(
                out=folded[:, :, first:last], in0=folded[:, :, first:last], scalar=2.0,
                in1=plain[:, 0:G, first:last], op0=ALU.min, op1=ALU.mult,
            )

        def join(u, reach_sum, scaled, result, first_sub, n_subs):
            k, bq = units[u]
            subs = slice(first_sub, first_sub + n_subs)
            nc.vector.scalar_tensor_tensor(
                out=result[:, subs, :], in0=reach_sum[:], scalar=-6.0,
                in1=scaled[:, subs, :], op0=ALU.mult, op1=ALU.add,
            )
            rows = slice(bq * N_COLS + first_sub * P, bq * N_COLS + (first_sub + n_subs) * P)
            nc.sync.dma_start(
                out=out[rows, k * P : (k + 1) * P].rearrange("(s p) i -> p s i", p=P),
                in_=result[:, subs, :],
            )

        g_loaded = {}
        w_loaded = {}
        g_loaded[0] = load_grad(0)
        w_loaded[0] = load_weights(0)
        load_x(1, 0, I)
        g_loaded[1] = load_grad(1)
        load_x(2, 0, I)
        g_loaded[2] = load_grad(2)
        load_x(3, 0, I)
        g_loaded[3] = load_grad(3)
        load_x(0, P, I)
        w_loaded[1] = load_weights(1)

        run_ends = {sum(POOL_RUNS[: j + 1]): POOL_RUNS[j] for j in range(len(POOL_RUNS))}
        x_banks = {}
        x_twices = {}
        foldeds = {}
        plains = {}
        hs = {}
        scaleds = {}
        results = {}

        with tc.manual_schedule(engines={mybir.EngineType.PE, mybir.EngineType.Pool}):
            for t in range(-2, n_units + 2):
                last_unit = n_units - 1
                if 0 <= t - 1 < n_units:
                    folded = foldeds[t - 1]
                    for g in range(G):
                        nc.scalar.activation(
                            out=folded[:, g, :], in_=folded[:, g, :], func=ACT.Abs,
                            bias=half_less_2_knots[:, g : g + 1], scale=1.0,
                        )
                if 0 <= t < n_units:
                    folded = foldeds[t]
                    plain = curves.tile([P, TERMS, N_COLS], F32, bufs=2)
                    plains[t] = plain
                    for g in range(G):
                        nc.vector.scalar_tensor_tensor(
                            out=plain[:, g, :], in0=folded[:, g, :], scalar=0.5, in1=hs[t, g][:],
                            op0=ALU.subtract, op1=ALU.mult,
                        )
                        if g + 1 in run_ends:
                            run = slice(g + 1 - run_ends[g + 1], g + 1)
                            nc.gpsimd.tensor_tensor(
                                out=folded[:, run, :],
                                in0=x_twices[t][:].unsqueeze(1).to_broadcast(
                                    [P, run_ends[g + 1], N_COLS]
                                ),
                                in1=folded[:, run, :],
                                op=ALU.subtract,
                            )
                        if g + H_BANKS < TERMS:
                            hs[t, g + H_BANKS] = mx_product(t, g + H_BANKS)
                    nc.vector.tensor_scalar_mul(
                        out=plain[:, G, :], in0=hs[t, G][:], scalar1=0.1 / 12.0
                    )
                if 0 <= t - 2 < last_unit:
                    reach_sum = sums.tile([P, SUB, P], F32)
                    sum_terms(reach_sum, foldeds[t - 2], G, 0, SUB)
                if t + 2 < n_units:
                    x_banks[t + 2] = turn_x(t + 2)
                if 0 <= t - 2 < last_unit:
                    results[t - 2] = curves.tile([P, SUB, P], F32, name="result")
                    join(t - 2, reach_sum, scaleds[t - 2], results[t - 2], 0, SUB)
                if t + 2 < n_units:
                    x_twices[t + 2] = copy_x(x_banks[t + 2])
                if 0 <= t < n_units:
                    nc.vector.tensor_tensor(
                        out=folded[:, POOL_KNOTS:G, :],
                        in0=x_twices[t][:].unsqueeze(1).to_broadcast([P, G - POOL_KNOTS, N_COLS]),
                        in1=folded[:, POOL_KNOTS:G, :],
                        op=ALU.subtract,
                    )
                    plain_sum = sums.tile([P, SUB, P], F32)
                    sum_terms(plain_sum, plain, TERMS, 0, SUB)
                    scaleds[t] = curves.tile([P, SUB, P], F32, name="scaled")
                    nc.scalar.mul(out=scaleds[t][:], in_=plain_sum[:], mul=12.0)
                if 0 <= t - 1 < last_unit:
                    last_product(foldeds[t - 1], plains[t - 1], 0, N_COLS)
                if t - 1 == last_unit:
                    results[last_unit] = curves.tile([P, SUB, P], F32, name="result")
                    piece_sums = {}
                    for s in range(SUB + 1):
                        if s < SUB:
                            last_product(foldeds[last_unit], plains[last_unit], s * P, (s + 1) * P)
                            piece_sum = banks.tile([P, 1, P], F32, tag="bank")
                            sum_terms(piece_sum, foldeds[last_unit], G, s, 1)
                            piece_sums[s] = piece_sum
                        if s >= 1:
                            join(
                                last_unit, piece_sums[s - 1], scaleds[last_unit],
                                results[last_unit], s - 1, 1,
                            )
                if t == -2:
                    quantise_grad(0, g_loaded[0])
                    quantise_weights(0, w_loaded[0])
                    w_loaded[2] = load_weights(2)
                if t == -1:
                    for bq in range(1, B_BLOCKS):
                        quantise_grad(bq, g_loaded[bq])
                if t >= 0 and (t + 2) % B_BLOCKS == 0 and t + 2 < n_units:
                    k = (t + 2) // B_BLOCKS
                    quantise_weights(k, w_loaded[k])
                    if k + 2 < I_BLOCKS:
                        w_loaded[k + 2] = load_weights(k + 2)
                if 0 <= t + 1 < n_units:
                    for term in range(H_BANKS):
                        hs[t + 1, term] = mx_product(t + 1, term)
                    foldeds[t + 1] = fold(x_twices[t + 1])
